import numpy as np
import ml_dtypes


def mxq(x, axis, fmt="e4m3"):
    dtype, down = {"e4m3": (ml_dtypes.float8_e4m3fn, 7), "e5m2": (ml_dtypes.float8_e5m2, 14)}[fmt]
    v = np.moveaxis(np.asarray(x, np.float32).astype(ml_dtypes.bfloat16).astype(np.float64), axis, -1)
    blocks = v.reshape(v.shape[:-1] + (-1, 32))
    amax = np.abs(blocks).max(-1, keepdims=True)
    byte = np.maximum(np.where(amax > 0, np.frexp(amax)[1] - 1 + 127, 0) - down, 1)
    scale = np.exp2(byte - 127.0)
    codes = (blocks / scale).astype(np.float32).astype(dtype).astype(np.float64)
    return np.moveaxis((codes * scale).reshape(v.shape), -1, axis)


WIDE = False


def mx_kscale(k):
    if not WIDE:
        return np.ones(k)
    levels = np.array([10, -10, 5, -5, 0])
    a = np.random.permutation(np.resize(levels, k // 512 * 4)).reshape(k // 512, 4)
    idx = np.arange(k)
    return np.exp2(a[idx // 512, idx % 128 // 32])


BF16 = ml_dtypes.bfloat16


def bf(x):
    return np.asarray(x, np.float32).astype(BF16)


def f64(x):
    return np.asarray(x).astype(np.float64)


B, N, E, H, C = 1, 1024, 2048, 8, 512
D = E // H
EPS = 1e-5


def silu(t):
    return t / (1.0 + np.exp(-t))


def setup_inputs():
    t = mx_kscale(E)
    ret = np.random.standard_normal((B, N, H, D)) * 4.0 + np.random.standard_normal((B, N, H, 1)) * 2.0
    return {"ret": bf(ret.reshape(B, N, E)),
            "g": bf(np.random.standard_normal((B, N, E))),
            "gn_weight": bf((1.0 + 0.1 * np.random.standard_normal(E)) * t),
            "gn_bias": bf(0.1 * np.random.standard_normal(E) * t),
            "w_o": bf(np.random.standard_normal((E, E)) / np.sqrt(E) / t[:, None]),
            "b_o": bf(np.random.standard_normal(E) * 0.3)}


def reference(ret, g, gn_weight, gn_bias, w_o, b_o):
    r = f64(ret).reshape(B, N, H, D)
    mean = r.mean(axis=-1, keepdims=True)
    var = r.var(axis=-1, keepdims=True)
    r = (r - mean) / np.sqrt(var + EPS)
    rn = r.reshape(B, N, E) * f64(gn_weight) + f64(gn_bias)
    gate = silu(f64(g)) * rn
    return (mxq(gate, 2, "e4m3") @ mxq(f64(w_o), 0, "e4m3")) + f64(b_o)

@@ -1,0 +1,289 @@
+from contextlib import ExitStack
+
+import concourse.mybir as mybir
+from concourse.masks import make_identity
+
+F32 = mybir.dt.float32
+BF16 = mybir.dt.bfloat16
+U32 = mybir.dt.uint32
+U8 = mybir.dt.uint8
+FP8X4 = mybir.dt.float8_e4m3fn_x4
+ACT = mybir.ActivationFunctionType
+ALU = mybir.AluOpType
+
+P = 128
+PACK = 4
+K_PASS = P * PACK
+TOKENS = 1024
+E = 2048
+D = 256
+HEADS_PER_PASS = K_PASS // D
+EPS = 1e-5
+PASSES = E // K_PASS
+K_BLOCKS = E // P
+N_TILE = 512
+N_TILES = E // N_TILE
+GROUP_TILES = 2
+GROUP_TOKENS = GROUP_TILES * P
+TOKEN_GROUPS = TOKENS // GROUP_TOKENS
+ROUNDS = TOKEN_GROUPS * PASSES
+W_PIECES = N_TILES * PASSES
+PIECES_PER_STEP = 2
+RAW_PIECES = 8
+STATS_AHEAD = 3
+VECTOR_COLS = 320
+
+FLOPS = 2 * TOKENS * E * E
+
+
+def tile_multiscaleretention_pc_kernel(tc, ret, g, gn_weight, gn_bias, w_o, b_o, out):
+    nc = tc.nc
+    ret_rows = ret.flatten_outer_dims()
+    g_rows = g.flatten_outer_dims()
+    out_rows = out.flatten_outer_dims()
+    w_view = w_o.rearrange("(c t p) n -> c p t n", t=PACK, p=P)
+
+    with ExitStack() as ctx:
+        consts = ctx.enter_context(tc.tile_pool(name="consts", bufs=1))
+        keep = ctx.enter_context(tc.tile_pool(name="keep", bufs=1))
+        token_pool = ctx.enter_context(tc.tile_pool(name="token_pool", bufs=TOKENS // P))
+        norm_pool = ctx.enter_context(tc.tile_pool(name="norm_pool", bufs=3))
+        small = ctx.enter_context(tc.tile_pool(name="small", bufs=STATS_AHEAD + 2))
+        kmajor = ctx.enter_context(tc.tile_pool(name="kmajor", bufs=2))
+        w_raw_pool = ctx.enter_context(tc.tile_pool(name="w_raw_pool", bufs=RAW_PIECES))
+        w_grouped_pool = ctx.enter_context(tc.tile_pool(name="w_grouped_pool", bufs=3))
+        out_pool = ctx.enter_context(tc.tile_pool(name="out_pool", bufs=4))
+        psum_norm = ctx.enter_context(tc.psum_pool(name="psum_norm", bufs=3))
+        psum_g = ctx.enter_context(tc.psum_pool(name="psum_g", bufs=2))
+        psum_acc = ctx.enter_context(tc.psum_pool(name="psum_acc", bufs=3))
+        ctx.enter_context(tc.manual_schedule())
+
+        w_codes = keep.tile([P, PASSES, E], U32, align_bytes=64)
+        w_scales = keep.tile([P, PASSES, E], U8, align_bytes=64)
+        gate_codes = keep.tile([P, PASSES, TOKENS], U32, align_bytes=64)
+        gate_scales = keep.tile([P, PASSES, TOKENS], U8, align_bytes=64)
+
+        ret_tiles = {}
+        g_tiles = {}
+        raw_tiles = {}
+
+        def load_tokens(rows_of, tiles, s, name):
+            for i in range(s * GROUP_TILES, (s + 1) * GROUP_TILES):
+                tiles[i] = token_pool.tile([P, E], BF16, name=name)
+                nc.sync.dma_start(out=tiles[i][:], in_=rows_of[i * P : (i + 1) * P, :])
+
+        def load_w_piece(k):
+            j, c = divmod(k, PASSES)
+            raw_tiles[k] = w_raw_pool.tile([P, PACK, N_TILE], BF16, name="raw")
+            nc.sync.dma_start(out=raw_tiles[k][:], in_=w_view[c, :, :, j * N_TILE : (j + 1) * N_TILE])
+
+        affine_rows = consts.tile([P, P], BF16)
+        nc.gpsimd.memset(affine_rows[:], 0.0)
+        load_tokens(ret_rows, ret_tiles, 0, "ret_t")
+        nc.sync.dma_start(out=affine_rows[0:K_BLOCKS, :], in_=gn_weight.rearrange("(b p) -> b p", p=P))
+        nc.sync.dma_start(out=affine_rows[K_BLOCKS : 2 * K_BLOCKS, :], in_=gn_bias.rearrange("(b p) -> b p", p=P))
+        load_w_piece(0)
+        load_w_piece(1)
+        load_tokens(g_rows, g_tiles, 0, "g_t")
+        load_w_piece(2)
+        load_w_piece(3)
+        load_tokens(ret_rows, ret_tiles, 1, "ret_t")
+        load_w_piece(4)
+        load_w_piece(5)
+        load_tokens(g_rows, g_tiles, 1, "g_t")
+        load_w_piece(6)
+        load_w_piece(7)
+
+        ident_f32 = consts.tile([P, P], F32)
+        make_identity(nc, ident_f32[:])
+        ident_bf16 = consts.tile([P, P], BF16)
+        make_identity(nc, ident_bf16[:])
+        neg_half = consts.tile([P, GROUP_TILES, HEADS_PER_PASS], F32)
+        nc.gpsimd.memset(neg_half[:], -0.5)
+        bias_all = consts.tile([P, E], BF16)
+        affine_cols = consts.tile([P, 2 * K_BLOCKS], F32)
+
+        rstd_of = {}
+        shift_of = {}
+        norm_of = {}
+        norm_T_of = {}
+        g_T_of = {}
+        rn_T_of = {}
+        silu_T_of = {}
+
+        def statistics(n):
+            if n >= ROUNDS:
+                return
+            s, c = divmod(n, PASSES)
+            stats = small.tile([P, GROUP_TILES, HEADS_PER_PASS, 3], F32, name="stats")
+            for r in range(GROUP_TILES):
+                two_heads = ret_tiles[s * GROUP_TILES + r][:, c * K_PASS : (c + 1) * K_PASS]
+                nc.vector.bn_stats(
+                    out=stats[:, r, :, :].rearrange("p h s -> p (h s)"),
+                    in_=two_heads.rearrange("p (h d) -> p d h", h=HEADS_PER_PASS),
+                )
+            neg_mean = small.tile([P, GROUP_TILES, HEADS_PER_PASS], F32, name="neg_mean")
+            nc.gpsimd.tensor_scalar(
+                out=neg_mean[:], in0=stats[:, :, :, 1], scalar1=-1.0, scalar2=0.0, op0=ALU.mult, op1=ALU.add
+            )
+            var_eps = small.tile([P, GROUP_TILES, HEADS_PER_PASS], F32, name="var_eps")
+            nc.gpsimd.tensor_scalar(
+                out=var_eps[:], in0=stats[:, :, :, 2], scalar1=1.0 / D, scalar2=EPS, op0=ALU.mult, op1=ALU.add
+            )
+            rstd = small.tile([P, GROUP_TILES, HEADS_PER_PASS], F32, name="rstd")
+            nc.gpsimd.tensor_tensor(out=rstd[:], in0=var_eps[:], in1=neg_half[:], op=ALU.pow)
+            shift = small.tile([P, GROUP_TILES, HEADS_PER_PASS], F32, name="shift")
+            nc.gpsimd.tensor_tensor(out=shift[:], in0=neg_mean[:], in1=rstd[:], op=ALU.mult)
+            rstd_of[n] = rstd
+            shift_of[n] = shift
+
+        def normalise(n):
+            if n >= ROUNDS:
+                return
+            s, c = divmod(n, PASSES)
+            norm = norm_pool.tile([P, GROUP_TILES, K_PASS], F32, name="norm")
+            for r in range(GROUP_TILES):
+                for h in range(HEADS_PER_PASS):
+                    nc.scalar.activation(
+                        out=norm[:, r, h * D : (h + 1) * D],
+                        in_=ret_tiles[s * GROUP_TILES + r][:, c * K_PASS + h * D : c * K_PASS + (h + 1) * D],
+                        func=ACT.Identity,
+                        scale=rstd_of[n][:, r, h : h + 1],
+                        bias=shift_of[n][:, r, h : h + 1],
+                    )
+            norm_of[n] = norm
+
+        def transposes(n):
+            if n >= ROUNDS:
+                return
+            s, c = divmod(n, PASSES)
+            norm_T = [
+                psum_norm.tile([P, 2, GROUP_TOKENS], F32, name="norm_T%d" % half, tag="norm_T") for half in range(2)
+            ]
+            for t in range(PACK):
+                for r in range(GROUP_TILES):
+                    nc.tensor.transpose(
+                        norm_T[t // 2][:, t % 2, r * P : (r + 1) * P], norm_of[n][:, r, t * P : (t + 1) * P], ident_f32[:]
+                    )
+            g_T = psum_g.tile([P, PACK, GROUP_TOKENS], BF16, name="g_T")
+            for t in range(PACK):
+                for r in range(GROUP_TILES):
+                    nc.tensor.transpose(
+                        g_T[:, t, r * P : (r + 1) * P],
+                        g_tiles[s * GROUP_TILES + r][:, c * K_PASS + t * P : c * K_PASS + (t + 1) * P],
+                        ident_bf16[:],
+                    )
+            norm_T_of[n] = norm_T
+            g_T_of[n] = g_T
+
+        def affine_and_silu(n):
+            if n >= ROUNDS:
+                return
+            c = n % PASSES
+            rn_T = kmajor.tile([P, PACK, GROUP_TOKENS], F32, name="rn_T")
+            for t in range(PACK):
+                b = c * PACK + t
+                nc.scalar.activation(
+                    out=rn_T[:, t, :], in_=norm_T_of[n][t // 2][:, t % 2, :], func=ACT.Identity,
+                    scale=affine_cols[:, b : b + 1], bias=affine_cols[:, K_BLOCKS + b : K_BLOCKS + b + 1],
+                )
+            silu_T = kmajor.tile([P, GROUP_TOKENS, PACK], F32, name="silu_T")
+            nc.scalar.activation(out=silu_T[:], in_=g_T_of[n][:].rearrange("p t r -> p r t"), func=ACT.Silu)
+            rn_T_of[n] = rn_T
+            silu_T_of[n] = silu_T
+
+        def gate_product(n):
+            if n < 0 or n >= ROUNDS:
+                return
+            s, c = divmod(n, PASSES)
+            gate_grouped = kmajor.tile([P, GROUP_TOKENS, PACK], BF16, name="gate_grouped", align_bytes=64)
+            nc.vector.tensor_tensor(
+                out=gate_grouped[:], in0=rn_T_of[n][:].rearrange("p t r -> p r t"), in1=silu_T_of[n][:], op=ALU.mult
+            )
+            tokens = slice(s * GROUP_TOKENS, (s + 1) * GROUP_TOKENS)
+            nc.vector.quantize_mx(
+                out=gate_codes[:, c, tokens].bitcast(FP8X4),
+                scales=gate_scales[:, c, tokens],
+                in_=gate_grouped[:].rearrange("p r t -> p (r t)"),
+            )
+
+        def quantise_w_pieces(first):
+            pieces = [k for k in range(first, first + PIECES_PER_STEP) if k < W_PIECES]
+            grouped_of = {}
+            v = VECTOR_COLS
+            for k in pieces:
+                grouped = w_grouped_pool.tile([P, N_TILE, PACK], BF16, name="grouped", align_bytes=64)
+                nc.vector.tensor_copy(
+                    out=grouped[:, 0:v, :].rearrange("p (n i) t -> p n t i", i=4),
+                    in_=raw_tiles[k][:, :, 0:v].rearrange("p t (n i) -> p n t i", i=4),
+                )
+                nc.scalar.copy(
+                    out=grouped[:, v:N_TILE, :].rearrange("p (n i) t -> p n t i", i=4),
+                    in_=raw_tiles[k][:, :, v:N_TILE].rearrange("p t (n i) -> p n t i", i=4),
+                )
+                grouped_of[k] = grouped
+            for k in pieces:
+                j, c = divmod(k, PASSES)
+                n_cols = slice(j * N_TILE, (j + 1) * N_TILE)
+                nc.vector.quantize_mx(
+                    out=w_codes[:, c, n_cols].bitcast(FP8X4),
+                    scales=w_scales[:, c, n_cols],
+                    in_=grouped_of[k][:].rearrange("p n t -> p (n t)"),
+                )
+
+        def multiply(s, j):
+            n_cols = slice(j * N_TILE, (j + 1) * N_TILE)
+            products = []
+            for i in range(s * GROUP_TILES, (s + 1) * GROUP_TILES):
+                tokens = slice(i * P, (i + 1) * P)
+                acc = psum_acc.tile([P, N_TILE], F32, name="acc")
+                for c in range(PASSES):
+                    nc.tensor.matmul_mx(
+                        out=acc[:],
+                        lhsT=gate_codes[:, c, tokens].bitcast(FP8X4),
+                        lhsT_scale=gate_scales[:, c, tokens],
+                        rhs=w_codes[:, c, n_cols].bitcast(FP8X4),
+                        rhs_scale=w_scales[:, c, n_cols],
+                        start=(c == 0),
+                        stop=(c == PASSES - 1),
+                    )
+                products.append((acc, tokens, n_cols))
+            return products
+
+        def add_bias_and_store(products):
+            for acc, tokens, n_cols in products:
+                result = out_pool.tile([P, N_TILE], F32, name="result")
+                nc.vector.tensor_tensor(out=result[:], in0=acc[:], in1=bias_all[:, n_cols], op=ALU.add)
+                nc.sync.dma_start(out=out_rows[tokens, n_cols], in_=result[:])
+
+        for n in range(STATS_AHEAD):
+            statistics(n)
+        affine_ps = psum_g.tile([P, PACK, GROUP_TOKENS], BF16, tag="g_T")
+        nc.tensor.transpose(affine_ps[:, 0, 0:P], affine_rows[:], ident_bf16[:])
+        nc.vector.tensor_copy(out=affine_cols[:], in_=affine_ps[:, 0, 0 : 2 * K_BLOCKS])
+        quantise_w_pieces(0)
+        normalise(0)
+
+        products = []
+        for n in range(ROUNDS + PASSES + 1):
+            statistics(n + STATS_AHEAD)
+            transposes(n)
+            normalise(n + 1)
+            affine_and_silu(n)
+            add_bias_and_store(products)
+            gate_product(n - 1)
+            first = (n + 1) * PIECES_PER_STEP
+            quantise_w_pieces(first)
+            for k in range(first - PIECES_PER_STEP + RAW_PIECES, first + RAW_PIECES):
+                if k < W_PIECES:
+                    load_w_piece(k)
+            if n == 0:
+                nc.sync.dma_start(out=bias_all[:], in_=b_o.partition_broadcast(P))
+            if n < 2 * (TOKEN_GROUPS - 2):
+                if n % 2 == 0:
+                    load_tokens(ret_rows, ret_tiles, 2 + n // 2, "ret_t")
+                else:
+                    load_tokens(g_rows, g_tiles, 2 + n // 2, "g_t")
+            m = n - 1 - PASSES
+            products = multiply(m // PASSES, m % PASSES) if m >= 0 else []
+        add_bias_and_store(products)

@@ -187,8 +187,8 @@ def tile_multiscaleretention_pc_kernel(tc, ret, g, gn_weight, gn_bias, w_o, b_o,
                     out=rn_T[:, t, :], in_=norm_T_of[n][t // 2][:, t % 2, :], func=ACT.Identity,
                     scale=affine_cols[:, b : b + 1], bias=affine_cols[:, K_BLOCKS + b : K_BLOCKS + b + 1],
                 )
-            silu_T = kmajor.tile([P, GROUP_TOKENS, PACK], F32, name="silu_T")
-            nc.scalar.activation(out=silu_T[:], in_=g_T_of[n][:].rearrange("p t r -> p r t"), func=ACT.Silu)
+            silu_T = kmajor.tile([P, PACK, GROUP_TOKENS], F32, name="silu_T")
+            nc.scalar.activation(out=silu_T[:], in_=g_T_of[n][:], func=ACT.Silu)
             rn_T_of[n] = rn_T
             silu_T_of[n] = silu_T
 
@@ -198,7 +198,10 @@ def tile_multiscaleretention_pc_kernel(tc, ret, g, gn_weight, gn_bias, w_o, b_o,
             s, c = divmod(n, PASSES)
             gate_grouped = kmajor.tile([P, GROUP_TOKENS, PACK], BF16, name="gate_grouped", align_bytes=64)
             nc.vector.tensor_tensor(
-                out=gate_grouped[:], in0=rn_T_of[n][:].rearrange("p t r -> p r t"), in1=silu_T_of[n][:], op=ALU.mult
+                out=gate_grouped[:].rearrange("p (n i) t -> p n t i", i=4),
+                in0=rn_T_of[n][:].rearrange("p t (n i) -> p n t i", i=4),
+                in1=silu_T_of[n][:].rearrange("p t (n i) -> p n t i", i=4),
+                op=ALU.mult,
             )
             tokens = slice(s * GROUP_TOKENS, (s + 1) * GROUP_TOKENS)
             nc.vector.quantize_mx(

@@ -153,10 +153,9 @@ def tile_multiscaleretention_pc_kernel(tc, ret, g, gn_weight, gn_bias, w_o, b_o,
                     )
             norm_of[n] = norm
 
-        def transposes(n):
+        def transpose_norm(n):
             if n >= ROUNDS:
                 return
-            s, c = divmod(n, PASSES)
             norm_T = [
                 psum_norm.tile([P, 2, GROUP_TOKENS], F32, name="norm_T%d" % half, tag="norm_T") for half in range(2)
             ]
@@ -165,6 +164,12 @@ def tile_multiscaleretention_pc_kernel(tc, ret, g, gn_weight, gn_bias, w_o, b_o,
                     nc.tensor.transpose(
                         norm_T[t // 2][:, t % 2, r * P : (r + 1) * P], norm_of[n][:, r, t * P : (t + 1) * P], ident_f32[:]
                     )
+            norm_T_of[n] = norm_T
+
+        def transpose_g(n):
+            if n >= ROUNDS:
+                return
+            s, c = divmod(n, PASSES)
             g_T = psum_g.tile([P, PACK, GROUP_TOKENS], BF16, name="g_T")
             for t in range(PACK):
                 for r in range(GROUP_TILES):
@@ -173,7 +178,6 @@ def tile_multiscaleretention_pc_kernel(tc, ret, g, gn_weight, gn_bias, w_o, b_o,
                         g_tiles[s * GROUP_TILES + r][:, c * K_PASS + t * P : c * K_PASS + (t + 1) * P],
                         ident_bf16[:],
                     )
-            norm_T_of[n] = norm_T
             g_T_of[n] = g_T
 
         def affine_and_silu(n):
@@ -234,24 +238,25 @@ def tile_multiscaleretention_pc_kernel(tc, ret, g, gn_weight, gn_bias, w_o, b_o,
                     in_=grouped_of[k][:].rearrange("p n t -> p (n t)"),
                 )
 
-        def multiply(s, j):
+        def multiply(m, r):
+            if m < 0 or m >= TOKEN_GROUPS * N_TILES:
+                return []
+            s, j = divmod(m, N_TILES)
             n_cols = slice(j * N_TILE, (j + 1) * N_TILE)
-            products = []
-            for i in range(s * GROUP_TILES, (s + 1) * GROUP_TILES):
-                tokens = slice(i * P, (i + 1) * P)
-                acc = psum_acc.tile([P, N_TILE], F32, name="acc")
-                for c in range(PASSES):
-                    nc.tensor.matmul_mx(
-                        out=acc[:],
-                        lhsT=gate_codes[:, c, tokens].bitcast(FP8X4),
-                        lhsT_scale=gate_scales[:, c, tokens],
-                        rhs=w_codes[:, c, n_cols].bitcast(FP8X4),
-                        rhs_scale=w_scales[:, c, n_cols],
-                        start=(c == 0),
-                        stop=(c == PASSES - 1),
-                    )
-                products.append((acc, tokens, n_cols))
-            return products
+            i = s * GROUP_TILES + r
+            tokens = slice(i * P, (i + 1) * P)
+            acc = psum_acc.tile([P, N_TILE], F32, name="acc")
+            for c in range(PASSES):
+                nc.tensor.matmul_mx(
+                    out=acc[:],
+                    lhsT=gate_codes[:, c, tokens].bitcast(FP8X4),
+                    lhsT_scale=gate_scales[:, c, tokens],
+                    rhs=w_codes[:, c, n_cols].bitcast(FP8X4),
+                    rhs_scale=w_scales[:, c, n_cols],
+                    start=(c == 0),
+                    stop=(c == PASSES - 1),
+                )
+            return [(acc, tokens, n_cols)]
 
         def add_bias_and_store(products):
             for acc, tokens, n_cols in products:
@@ -267,10 +272,13 @@ def tile_multiscaleretention_pc_kernel(tc, ret, g, gn_weight, gn_bias, w_o, b_o,
         quantise_w_pieces(0)
         normalise(0)
 
-        products = []
-        for n in range(ROUNDS + PASSES + 1):
+        for n in range(ROUNDS + PASSES + 2):
             statistics(n + STATS_AHEAD)
-            transposes(n)
+            m = n - 2 - PASSES
+            transpose_norm(n)
+            products = multiply(m, 0)
+            transpose_g(n)
+            products = products + multiply(m, 1)
             normalise(n + 1)
             affine_and_silu(n)
             add_bias_and_store(products)
@@ -287,6 +295,3 @@ def tile_multiscaleretention_pc_kernel(tc, ret, g, gn_weight, gn_bias, w_o, b_o,
                     load_tokens(ret_rows, ret_tiles, 2 + n // 2, "ret_t")
                 else:
                     load_tokens(g_rows, g_tiles, 2 + n // 2, "g_t")
-            m = n - 1 - PASSES
-            products = multiply(m // PASSES, m % PASSES) if m >= 0 else []
-        add_bias_and_store(products)

@@ -13,25 +13,33 @@ ALU = mybir.AluOpType
 
 P = 128
 PACK = 4
+PAIR = 2
+HALVES = PACK // PAIR
 K_PASS = P * PACK
 TOKENS = 1024
+TOKEN_TILES = TOKENS // P
 E = 2048
 D = 256
-HEADS_PER_PASS = K_PASS // D
 EPS = 1e-5
 PASSES = E // K_PASS
 K_BLOCKS = E // P
+HEADS = E // D
 N_TILE = 512
-N_TILES = E // N_TILE
-GROUP_TILES = 2
-GROUP_TOKENS = GROUP_TILES * P
-TOKEN_GROUPS = TOKENS // GROUP_TOKENS
-ROUNDS = TOKEN_GROUPS * PASSES
-W_PIECES = N_TILES * PASSES
+ROUND_PASSES = 2
+ROUND_K = ROUND_PASSES * K_PASS
+ROUND_HEADS = ROUND_K // D
+TILE_ROUNDS = PASSES // ROUND_PASSES
+ROUNDS = TOKEN_TILES * TILE_ROUNDS
+WORDS = ROUND_PASSES * P
+W_COLS = 1024
+W_PIECES = (E // W_COLS) * PASSES
 PIECES_PER_STEP = 2
-RAW_PIECES = 8
+RAW_PIECES = 4
+UNIT_TILES = W_COLS // N_TILE
+UNITS = TOKEN_TILES * (E // W_COLS)
 STATS_AHEAD = 3
-VECTOR_COLS = 320
+UNIT_LAG = 3
+VECTOR_COLS = 512
 
 FLOPS = 2 * TOKENS * E * E
 
@@ -41,12 +49,12 @@ def tile_multiscaleretention_pc_kernel(tc, ret, g, gn_weight, gn_bias, w_o, b_o,
     ret_rows = ret.flatten_outer_dims()
     g_rows = g.flatten_outer_dims()
     out_rows = out.flatten_outer_dims()
-    w_view = w_o.rearrange("(c t p) n -> c p t n", t=PACK, p=P)
+    w_view = w_o.rearrange("(c u q e) n -> c u q e n", u=HALVES, q=P, e=PAIR)
 
     with ExitStack() as ctx:
         consts = ctx.enter_context(tc.tile_pool(name="consts", bufs=1))
         keep = ctx.enter_context(tc.tile_pool(name="keep", bufs=1))
-        token_pool = ctx.enter_context(tc.tile_pool(name="token_pool", bufs=TOKENS // P))
+        token_pool = ctx.enter_context(tc.tile_pool(name="token_pool", bufs=TOKEN_TILES))
         norm_pool = ctx.enter_context(tc.tile_pool(name="norm_pool", bufs=3))
         small = ctx.enter_context(tc.tile_pool(name="small", bufs=STATS_AHEAD + 2))
         kmajor = ctx.enter_context(tc.tile_pool(name="kmajor", bufs=2))
@@ -60,45 +68,46 @@ def tile_multiscaleretention_pc_kernel(tc, ret, g, gn_weight, gn_bias, w_o, b_o,
 
         w_codes = keep.tile([P, PASSES, E], U32, align_bytes=64)
         w_scales = keep.tile([P, PASSES, E], U8, align_bytes=64)
-        gate_codes = keep.tile([P, PASSES, TOKENS], U32, align_bytes=64)
-        gate_scales = keep.tile([P, PASSES, TOKENS], U8, align_bytes=64)
+        gate_codes = keep.tile([P, ROUNDS, WORDS], U32, align_bytes=64)
+        gate_scales = keep.tile([P, ROUNDS, WORDS], U8, align_bytes=64)
 
         ret_tiles = {}
         g_tiles = {}
         raw_tiles = {}
+        grouped_tiles = {}
 
-        def load_tokens(rows_of, tiles, s, name):
-            for i in range(s * GROUP_TILES, (s + 1) * GROUP_TILES):
+        def load_tokens(rows_of, tiles, i, name):
+            if i < TOKEN_TILES:
                 tiles[i] = token_pool.tile([P, E], BF16, name=name)
                 nc.sync.dma_start(out=tiles[i][:], in_=rows_of[i * P : (i + 1) * P, :])
 
         def load_w_piece(k):
-            j, c = divmod(k, PASSES)
-            raw_tiles[k] = w_raw_pool.tile([P, PACK, N_TILE], BF16, name="raw")
-            nc.sync.dma_start(out=raw_tiles[k][:], in_=w_view[c, :, :, j * N_TILE : (j + 1) * N_TILE])
+            if k < W_PIECES:
+                jj, c = divmod(k, PASSES)
+                raw_tiles[k] = w_raw_pool.tile([P, PACK, W_COLS], BF16, name="raw")
+                for u in range(HALVES):
+                    nc.sync.dma_start(
+                        out=raw_tiles[k][:, u * PAIR : (u + 1) * PAIR, :],
+                        in_=w_view[c, u, :, :, jj * W_COLS : (jj + 1) * W_COLS],
+                    )
 
-        affine_rows = consts.tile([P, P], BF16)
+        affine_rows = consts.tile([P, D], BF16)
         nc.gpsimd.memset(affine_rows[:], 0.0)
         load_tokens(ret_rows, ret_tiles, 0, "ret_t")
-        nc.sync.dma_start(out=affine_rows[0:K_BLOCKS, :], in_=gn_weight.rearrange("(b p) -> b p", p=P))
-        nc.sync.dma_start(out=affine_rows[K_BLOCKS : 2 * K_BLOCKS, :], in_=gn_bias.rearrange("(b p) -> b p", p=P))
+        load_tokens(ret_rows, ret_tiles, 1, "ret_t")
+        load_tokens(g_rows, g_tiles, 0, "g_t")
+        nc.sync.dma_start(out=affine_rows[0:HEADS, :], in_=gn_weight.rearrange("(b x) -> b x", x=D))
+        nc.sync.dma_start(out=affine_rows[HEADS : 2 * HEADS, :], in_=gn_bias.rearrange("(b x) -> b x", x=D))
         load_w_piece(0)
         load_w_piece(1)
-        load_tokens(g_rows, g_tiles, 0, "g_t")
+        load_tokens(ret_rows, ret_tiles, 2, "ret_t")
         load_w_piece(2)
         load_w_piece(3)
-        load_tokens(ret_rows, ret_tiles, 1, "ret_t")
-        load_w_piece(4)
-        load_w_piece(5)
         load_tokens(g_rows, g_tiles, 1, "g_t")
-        load_w_piece(6)
-        load_w_piece(7)
 
         ident_f32 = consts.tile([P, P], F32)
         make_identity(nc, ident_f32[:])
-        ident_bf16 = consts.tile([P, P], BF16)
-        make_identity(nc, ident_bf16[:])
-        neg_half = consts.tile([P, GROUP_TILES, HEADS_PER_PASS], F32)
+        neg_half = consts.tile([P, ROUND_HEADS], F32)
         nc.gpsimd.memset(neg_half[:], -0.5)
         bias_all = consts.tile([P, E], BF16)
         affine_cols = consts.tile([P, 2 * K_BLOCKS], F32)
@@ -110,29 +119,30 @@ def tile_multiscaleretention_pc_kernel(tc, ret, g, gn_weight, gn_bias, w_o, b_o,
         g_T_of = {}
         rn_T_of = {}
         silu_T_of = {}
+        gate_grouped_of = {}
 
         def statistics(n):
             if n >= ROUNDS:
                 return
-            s, c = divmod(n, PASSES)
-            stats = small.tile([P, GROUP_TILES, HEADS_PER_PASS, 3], F32, name="stats")
-            for r in range(GROUP_TILES):
-                two_heads = ret_tiles[s * GROUP_TILES + r][:, c * K_PASS : (c + 1) * K_PASS]
+            i, half = divmod(n, TILE_ROUNDS)
+            stats = small.tile([P, ROUND_HEADS, 3], F32, name="stats")
+            for first_head in range(0, ROUND_HEADS, 2):
+                first_col = half * ROUND_K + first_head * D
                 nc.vector.bn_stats(
-                    out=stats[:, r, :, :].rearrange("p h s -> p (h s)"),
-                    in_=two_heads.rearrange("p (h d) -> p d h", h=HEADS_PER_PASS),
+                    out=stats[:, first_head : first_head + 2, :].rearrange("p h s -> p (h s)"),
+                    in_=ret_tiles[i][:, first_col : first_col + 2 * D].rearrange("p (h d) -> p d h", h=2),
                 )
-            neg_mean = small.tile([P, GROUP_TILES, HEADS_PER_PASS], F32, name="neg_mean")
+            neg_mean = small.tile([P, ROUND_HEADS], F32, name="neg_mean")
             nc.gpsimd.tensor_scalar(
-                out=neg_mean[:], in0=stats[:, :, :, 1], scalar1=-1.0, scalar2=0.0, op0=ALU.mult, op1=ALU.add
+                out=neg_mean[:], in0=stats[:, :, 1], scalar1=-1.0, scalar2=0.0, op0=ALU.mult, op1=ALU.add
             )
-            var_eps = small.tile([P, GROUP_TILES, HEADS_PER_PASS], F32, name="var_eps")
+            var_eps = small.tile([P, ROUND_HEADS], F32, name="var_eps")
             nc.gpsimd.tensor_scalar(
-                out=var_eps[:], in0=stats[:, :, :, 2], scalar1=1.0 / D, scalar2=EPS, op0=ALU.mult, op1=ALU.add
+                out=var_eps[:], in0=stats[:, :, 2], scalar1=1.0 / D, scalar2=EPS, op0=ALU.mult, op1=ALU.add
             )
-            rstd = small.tile([P, GROUP_TILES, HEADS_PER_PASS], F32, name="rstd")
+            rstd = small.tile([P, ROUND_HEADS], F32, name="rstd")
             nc.gpsimd.tensor_tensor(out=rstd[:], in0=var_eps[:], in1=neg_half[:], op=ALU.pow)
-            shift = small.tile([P, GROUP_TILES, HEADS_PER_PASS], F32, name="shift")
+            shift = small.tile([P, ROUND_HEADS], F32, name="shift")
             nc.gpsimd.tensor_tensor(out=shift[:], in0=neg_mean[:], in1=rstd[:], op=ALU.mult)
             rstd_of[n] = rstd
             shift_of[n] = shift
@@ -140,123 +150,131 @@ def tile_multiscaleretention_pc_kernel(tc, ret, g, gn_weight, gn_bias, w_o, b_o,
         def normalise(n):
             if n >= ROUNDS:
                 return
-            s, c = divmod(n, PASSES)
-            norm = norm_pool.tile([P, GROUP_TILES, K_PASS], F32, name="norm")
-            for r in range(GROUP_TILES):
-                for h in range(HEADS_PER_PASS):
-                    nc.scalar.activation(
-                        out=norm[:, r, h * D : (h + 1) * D],
-                        in_=ret_tiles[s * GROUP_TILES + r][:, c * K_PASS + h * D : c * K_PASS + (h + 1) * D],
-                        func=ACT.Identity,
-                        scale=rstd_of[n][:, r, h : h + 1],
-                        bias=shift_of[n][:, r, h : h + 1],
-                    )
+            i, half = divmod(n, TILE_ROUNDS)
+            norm = norm_pool.tile([P, ROUND_HEADS, PAIR, P], F32, name="norm")
+            for h in range(ROUND_HEADS):
+                first_col = half * ROUND_K + h * D
+                nc.scalar.activation(
+                    out=norm[:, h, :, :],
+                    in_=ret_tiles[i][:, first_col : first_col + D].rearrange("p (q e) -> p e q", e=PAIR),
+                    func=ACT.Identity,
+                    scale=rstd_of[n][:, h : h + 1],
+                    bias=shift_of[n][:, h : h + 1],
+                )
             norm_of[n] = norm
 
-        def transpose_norm(n):
+        def transposes(n):
             if n >= ROUNDS:
                 return
-            norm_T = [
-                psum_norm.tile([P, 2, GROUP_TOKENS], F32, name="norm_T%d" % half, tag="norm_T") for half in range(2)
-            ]
-            for t in range(PACK):
-                for r in range(GROUP_TILES):
+            i, half = divmod(n, TILE_ROUNDS)
+            norm_T = [psum_norm.tile([P, PACK, P], F32, name="norm_T%d" % cr, tag="norm_T") for cr in range(ROUND_PASSES)]
+            for cr in range(ROUND_PASSES):
+                for t in range(PACK):
+                    u, e = divmod(t, PAIR)
+                    nc.tensor.transpose(norm_T[cr][:, t, :], norm_of[n][:, cr * HALVES + u, e, :], ident_f32[:])
+            g_T = psum_g.tile([P, HALVES * WORDS], F32, name="g_T")
+            g_words = g_tiles[i][:].bitcast(F32)
+            for u in range(HALVES):
+                for cr in range(ROUND_PASSES):
+                    first_word = (half * ROUND_K + (cr * HALVES + u) * D) // PAIR
                     nc.tensor.transpose(
-                        norm_T[t // 2][:, t % 2, r * P : (r + 1) * P], norm_of[n][:, r, t * P : (t + 1) * P], ident_f32[:]
+                        g_T[:, u * WORDS + cr * P : u * WORDS + (cr + 1) * P],
+                        g_words[:, first_word : first_word + P],
+                        ident_f32[:],
                     )
             norm_T_of[n] = norm_T
-
-        def transpose_g(n):
-            if n >= ROUNDS:
-                return
-            s, c = divmod(n, PASSES)
-            g_T = psum_g.tile([P, PACK, GROUP_TOKENS], BF16, name="g_T")
-            for t in range(PACK):
-                for r in range(GROUP_TILES):
-                    nc.tensor.transpose(
-                        g_T[:, t, r * P : (r + 1) * P],
-                        g_tiles[s * GROUP_TILES + r][:, c * K_PASS + t * P : c * K_PASS + (t + 1) * P],
-                        ident_bf16[:],
-                    )
             g_T_of[n] = g_T
 
         def affine_and_silu(n):
             if n >= ROUNDS:
                 return
-            c = n % PASSES
-            rn_T = kmajor.tile([P, PACK, GROUP_TOKENS], F32, name="rn_T")
-            for t in range(PACK):
-                b = c * PACK + t
-                nc.scalar.activation(
-                    out=rn_T[:, t, :], in_=norm_T_of[n][t // 2][:, t % 2, :], func=ACT.Identity,
-                    scale=affine_cols[:, b : b + 1], bias=affine_cols[:, K_BLOCKS + b : K_BLOCKS + b + 1],
-                )
-            silu_T = kmajor.tile([P, PACK, GROUP_TOKENS], F32, name="silu_T")
-            nc.scalar.activation(out=silu_T[:], in_=g_T_of[n][:], func=ACT.Silu)
+            half = n % TILE_ROUNDS
+            rn_T = kmajor.tile([P, PACK, WORDS], F32, name="rn_T")
+            for cr in range(ROUND_PASSES):
+                for t in range(PACK):
+                    b = (half * ROUND_PASSES + cr) * PACK + t
+                    nc.scalar.activation(
+                        out=rn_T[:, t, cr * P : (cr + 1) * P], in_=norm_T_of[n][cr][:, t, :], func=ACT.Identity,
+                        scale=affine_cols[:, b : b + 1], bias=affine_cols[:, K_BLOCKS + b : K_BLOCKS + b + 1],
+                    )
+            silu_T = kmajor.tile([P, PACK, WORDS], F32, name="silu_T")
+            nc.scalar.activation(
+                out=silu_T[:].rearrange("p (u e) x -> p u e x", e=PAIR),
+                in_=g_T_of[n][:].bitcast(BF16).rearrange("p (u x e) -> p u e x", u=HALVES, e=PAIR),
+                func=ACT.Silu,
+            )
             rn_T_of[n] = rn_T
             silu_T_of[n] = silu_T
 
         def gate_product(n):
             if n < 0 or n >= ROUNDS:
                 return
-            s, c = divmod(n, PASSES)
-            gate_grouped = kmajor.tile([P, GROUP_TOKENS, PACK], BF16, name="gate_grouped", align_bytes=64)
+            gate_grouped = kmajor.tile([P, WORDS, PACK], BF16, name="gate_grouped", align_bytes=64)
             nc.vector.tensor_tensor(
                 out=gate_grouped[:].rearrange("p (n i) t -> p n t i", i=4),
                 in0=rn_T_of[n][:].rearrange("p t (n i) -> p n t i", i=4),
                 in1=silu_T_of[n][:].rearrange("p t (n i) -> p n t i", i=4),
                 op=ALU.mult,
             )
-            tokens = slice(s * GROUP_TOKENS, (s + 1) * GROUP_TOKENS)
+            gate_grouped_of[n] = gate_grouped
+
+        def quantise_gate(n):
+            if n < 0 or n >= ROUNDS:
+                return
             nc.vector.quantize_mx(
-                out=gate_codes[:, c, tokens].bitcast(FP8X4),
-                scales=gate_scales[:, c, tokens],
-                in_=gate_grouped[:].rearrange("p r t -> p (r t)"),
+                out=gate_codes[:, n, :].bitcast(FP8X4),
+                scales=gate_scales[:, n, :],
+                in_=gate_grouped_of[n][:].rearrange("p x t -> p (x t)"),
             )
 
-        def quantise_w_pieces(first):
-            pieces = [k for k in range(first, first + PIECES_PER_STEP) if k < W_PIECES]
-            grouped_of = {}
+        def regroup_w_piece(k):
+            if k >= W_PIECES:
+                return
             v = VECTOR_COLS
-            for k in pieces:
-                grouped = w_grouped_pool.tile([P, N_TILE, PACK], BF16, name="grouped", align_bytes=64)
-                nc.vector.tensor_copy(
-                    out=grouped[:, 0:v, :].rearrange("p (n i) t -> p n t i", i=4),
-                    in_=raw_tiles[k][:, :, 0:v].rearrange("p t (n i) -> p n t i", i=4),
-                )
-                nc.scalar.copy(
-                    out=grouped[:, v:N_TILE, :].rearrange("p (n i) t -> p n t i", i=4),
-                    in_=raw_tiles[k][:, :, v:N_TILE].rearrange("p t (n i) -> p n t i", i=4),
-                )
-                grouped_of[k] = grouped
-            for k in pieces:
-                j, c = divmod(k, PASSES)
-                n_cols = slice(j * N_TILE, (j + 1) * N_TILE)
-                nc.vector.quantize_mx(
-                    out=w_codes[:, c, n_cols].bitcast(FP8X4),
-                    scales=w_scales[:, c, n_cols],
-                    in_=grouped_of[k][:].rearrange("p n t -> p (n t)"),
-                )
+            grouped = w_grouped_pool.tile([P, W_COLS, PACK], BF16, name="grouped", align_bytes=64)
+            nc.vector.tensor_copy(
+                out=grouped[:, 0:v, :].rearrange("p (n i) t -> p n t i", i=4),
+                in_=raw_tiles[k][:, :, 0:v].rearrange("p t (n i) -> p n t i", i=4),
+            )
+            nc.scalar.copy(
+                out=grouped[:, v:W_COLS, :].rearrange("p (n i) t -> p n t i", i=4),
+                in_=raw_tiles[k][:, :, v:W_COLS].rearrange("p t (n i) -> p n t i", i=4),
+            )
+            grouped_tiles[k] = grouped
 
-        def multiply(m, r):
-            if m < 0 or m >= TOKEN_GROUPS * N_TILES:
+        def quantise_w_piece(k):
+            if k < 0 or k >= W_PIECES:
+                return
+            jj, c = divmod(k, PASSES)
+            n_cols = slice(jj * W_COLS, (jj + 1) * W_COLS)
+            nc.vector.quantize_mx(
+                out=w_codes[:, c, n_cols].bitcast(FP8X4),
+                scales=w_scales[:, c, n_cols],
+                in_=grouped_tiles[k][:].rearrange("p n t -> p (n t)"),
+            )
+
+        def multiply(m):
+            if m < 0 or m >= UNITS:
                 return []
-            s, j = divmod(m, N_TILES)
-            n_cols = slice(j * N_TILE, (j + 1) * N_TILE)
-            i = s * GROUP_TILES + r
-            tokens = slice(i * P, (i + 1) * P)
-            acc = psum_acc.tile([P, N_TILE], F32, name="acc")
-            for c in range(PASSES):
-                nc.tensor.matmul_mx(
-                    out=acc[:],
-                    lhsT=gate_codes[:, c, tokens].bitcast(FP8X4),
-                    lhsT_scale=gate_scales[:, c, tokens],
-                    rhs=w_codes[:, c, n_cols].bitcast(FP8X4),
-                    rhs_scale=w_scales[:, c, n_cols],
-                    start=(c == 0),
-                    stop=(c == PASSES - 1),
-                )
-            return [(acc, tokens, n_cols)]
+            i, jj = divmod(m, E // W_COLS)
+            products = []
+            for j in range(jj * UNIT_TILES, (jj + 1) * UNIT_TILES):
+                n_cols = slice(j * N_TILE, (j + 1) * N_TILE)
+                acc = psum_acc.tile([P, N_TILE], F32, name="acc")
+                for c in range(PASSES):
+                    half, cr = divmod(c, ROUND_PASSES)
+                    made_in = i * TILE_ROUNDS + half
+                    nc.tensor.matmul_mx(
+                        out=acc[:],
+                        lhsT=gate_codes[:, made_in, cr * P : (cr + 1) * P].bitcast(FP8X4),
+                        lhsT_scale=gate_scales[:, made_in, cr * P : (cr + 1) * P],
+                        rhs=w_codes[:, c, n_cols].bitcast(FP8X4),
+                        rhs_scale=w_scales[:, c, n_cols],
+                        start=(c == 0),
+                        stop=(c == PASSES - 1),
+                    )
+                products.append((acc, slice(i * P, (i + 1) * P), n_cols))
+            return products
 
         def add_bias_and_store(products):
             for acc, tokens, n_cols in products:
@@ -266,32 +284,29 @@ def tile_multiscaleretention_pc_kernel(tc, ret, g, gn_weight, gn_bias, w_o, b_o,
 
         for n in range(STATS_AHEAD):
             statistics(n)
-        affine_ps = psum_g.tile([P, PACK, GROUP_TOKENS], BF16, tag="g_T")
-        nc.tensor.transpose(affine_ps[:, 0, 0:P], affine_rows[:], ident_bf16[:])
-        nc.vector.tensor_copy(out=affine_cols[:], in_=affine_ps[:, 0, 0 : 2 * K_BLOCKS])
-        quantise_w_pieces(0)
+        affine_ps = psum_g.tile([P, HALVES * WORDS], F32, tag="g_T")
+        nc.tensor.transpose(affine_ps[:, 0:P], affine_rows[:].bitcast(F32), ident_f32[:])
+        nc.vector.tensor_copy(out=affine_cols[:], in_=affine_ps[:, 0 : 2 * HEADS].bitcast(BF16))
         normalise(0)
 
-        for n in range(ROUNDS + PASSES + 2):
+        products = []
+        for n in range(ROUNDS + UNIT_LAG + 1):
             statistics(n + STATS_AHEAD)
-            m = n - 2 - PASSES
-            transpose_norm(n)
-            products = multiply(m, 0)
-            transpose_g(n)
-            products = products + multiply(m, 1)
+            transposes(n)
             normalise(n + 1)
             affine_and_silu(n)
-            add_bias_and_store(products)
             gate_product(n - 1)
-            first = (n + 1) * PIECES_PER_STEP
-            quantise_w_pieces(first)
-            for k in range(first - PIECES_PER_STEP + RAW_PIECES, first + RAW_PIECES):
-                if k < W_PIECES:
-                    load_w_piece(k)
-            if n == 0:
+            add_bias_and_store(products)
+            quantise_gate(n - 1)
+            first = n * PIECES_PER_STEP
+            for k in range(first - PIECES_PER_STEP, first):
+                quantise_w_piece(k)
+            for k in range(first, first + PIECES_PER_STEP):
+                regroup_w_piece(k)
+            for k in range(first + RAW_PIECES, first + RAW_PIECES + PIECES_PER_STEP):
+                load_w_piece(k)
+            load_tokens(ret_rows, ret_tiles, n + 3, "ret_t")
+            load_tokens(g_rows, g_tiles, n + 2, "g_t")
+            if n == 1:
                 nc.sync.dma_start(out=bias_all[:], in_=b_o.partition_broadcast(P))
-            if n < 2 * (TOKEN_GROUPS - 2):
-                if n % 2 == 0:
-                    load_tokens(ret_rows, ret_tiles, 2 + n // 2, "ret_t")
-                else:
-                    load_tokens(g_rows, g_tiles, 2 + n // 2, "g_t")
+            products = multiply(n - UNIT_LAG)

@@ -39,7 +39,7 @@ UNIT_TILES = W_COLS // N_TILE
 UNITS = TOKEN_TILES * (E // W_COLS)
 STATS_AHEAD = 3
 UNIT_LAG = 3
-VECTOR_COLS = 512
+VECTOR_COLS = 608
 
 FLOPS = 2 * TOKENS * E * E
 

from contextlib import ExitStack

import concourse.mybir as mybir
from concourse.masks import make_identity

F32 = mybir.dt.float32
BF16 = mybir.dt.bfloat16
U32 = mybir.dt.uint32
U8 = mybir.dt.uint8
FP8X4 = mybir.dt.float8_e4m3fn_x4
ACT = mybir.ActivationFunctionType
ALU = mybir.AluOpType

P = 128
PACK = 4
PAIR = 2
HALVES = PACK // PAIR
K_PASS = P * PACK
TOKENS = 1024
TOKEN_TILES = TOKENS // P
E = 2048
D = 256
EPS = 1e-5
PASSES = E // K_PASS
K_BLOCKS = E // P
HEADS = E // D
N_TILE = 512
ROUND_PASSES = 2
ROUND_K = ROUND_PASSES * K_PASS
ROUND_HEADS = ROUND_K // D
TILE_ROUNDS = PASSES // ROUND_PASSES
ROUNDS = TOKEN_TILES * TILE_ROUNDS
WORDS = ROUND_PASSES * P
W_COLS = 1024
W_PIECES = (E // W_COLS) * PASSES
PIECES_PER_STEP = 2
RAW_PIECES = 4
UNIT_TILES = W_COLS // N_TILE
UNITS = TOKEN_TILES * (E // W_COLS)
STATS_AHEAD = 3
UNIT_LAG = 3
VECTOR_COLS = 608

FLOPS = 2 * TOKENS * E * E


def tile_multiscaleretention_pc_kernel(tc, ret, g, gn_weight, gn_bias, w_o, b_o, out):
    nc = tc.nc
    ret_rows = ret.flatten_outer_dims()
    g_rows = g.flatten_outer_dims()
    out_rows = out.flatten_outer_dims()
    w_view = w_o.rearrange("(c u q e) n -> c u q e n", u=HALVES, q=P, e=PAIR)

    with ExitStack() as ctx:
        consts = ctx.enter_context(tc.tile_pool(name="consts", bufs=1))
        keep = ctx.enter_context(tc.tile_pool(name="keep", bufs=1))
        token_pool = ctx.enter_context(tc.tile_pool(name="token_pool", bufs=TOKEN_TILES))
        norm_pool = ctx.enter_context(tc.tile_pool(name="norm_pool", bufs=3))
        small = ctx.enter_context(tc.tile_pool(name="small", bufs=STATS_AHEAD + 2))
        kmajor = ctx.enter_context(tc.tile_pool(name="kmajor", bufs=2))
        w_raw_pool = ctx.enter_context(tc.tile_pool(name="w_raw_pool", bufs=RAW_PIECES))
        w_grouped_pool = ctx.enter_context(tc.tile_pool(name="w_grouped_pool", bufs=3))
        out_pool = ctx.enter_context(tc.tile_pool(name="out_pool", bufs=4))
        psum_norm = ctx.enter_context(tc.psum_pool(name="psum_norm", bufs=3))
        psum_g = ctx.enter_context(tc.psum_pool(name="psum_g", bufs=2))
        psum_acc = ctx.enter_context(tc.psum_pool(name="psum_acc", bufs=3))
        ctx.enter_context(tc.manual_schedule())

        w_codes = keep.tile([P, PASSES, E], U32, align_bytes=64)
        w_scales = keep.tile([P, PASSES, E], U8, align_bytes=64)
        gate_codes = keep.tile([P, ROUNDS, WORDS], U32, align_bytes=64)
        gate_scales = keep.tile([P, ROUNDS, WORDS], U8, align_bytes=64)

        ret_tiles = {}
        g_tiles = {}
        raw_tiles = {}
        grouped_tiles = {}

        def load_tokens(rows_of, tiles, i, name):
            if i < TOKEN_TILES:
                tiles[i] = token_pool.tile([P, E], BF16, name=name)
                nc.sync.dma_start(out=tiles[i][:], in_=rows_of[i * P : (i + 1) * P, :])

        def load_w_piece(k):
            if k < W_PIECES:
                jj, c = divmod(k, PASSES)
                raw_tiles[k] = w_raw_pool.tile([P, PACK, W_COLS], BF16, name="raw")
                for u in range(HALVES):
                    nc.sync.dma_start(
                        out=raw_tiles[k][:, u * PAIR : (u + 1) * PAIR, :],
                        in_=w_view[c, u, :, :, jj * W_COLS : (jj + 1) * W_COLS],
                    )

        affine_rows = consts.tile([P, D], BF16)
        nc.gpsimd.memset(affine_rows[:], 0.0)
        load_tokens(ret_rows, ret_tiles, 0, "ret_t")
        load_tokens(ret_rows, ret_tiles, 1, "ret_t")
        load_tokens(g_rows, g_tiles, 0, "g_t")
        nc.sync.dma_start(out=affine_rows[0:HEADS, :], in_=gn_weight.rearrange("(b x) -> b x", x=D))
        nc.sync.dma_start(out=affine_rows[HEADS : 2 * HEADS, :], in_=gn_bias.rearrange("(b x) -> b x", x=D))
        load_w_piece(0)
        load_w_piece(1)
        load_tokens(ret_rows, ret_tiles, 2, "ret_t")
        load_w_piece(2)
        load_w_piece(3)
        load_tokens(g_rows, g_tiles, 1, "g_t")

        ident_f32 = consts.tile([P, P], F32)
        make_identity(nc, ident_f32[:])
        neg_half = consts.tile([P, ROUND_HEADS], F32)
        nc.gpsimd.memset(neg_half[:], -0.5)
        bias_all = consts.tile([P, E], BF16)
        affine_cols = consts.tile([P, 2 * K_BLOCKS], F32)

        rstd_of = {}
        shift_of = {}
        norm_of = {}
        norm_T_of = {}
        g_T_of = {}
        rn_T_of = {}
        silu_T_of = {}
        gate_grouped_of = {}

        def statistics(n):
            if n >= ROUNDS:
                return
            i, half = divmod(n, TILE_ROUNDS)
            stats = small.tile([P, ROUND_HEADS, 3], F32, name="stats")
            for first_head in range(0, ROUND_HEADS, 2):
                first_col = half * ROUND_K + first_head * D
                nc.vector.bn_stats(
                    out=stats[:, first_head : first_head + 2, :].rearrange("p h s -> p (h s)"),
                    in_=ret_tiles[i][:, first_col : first_col + 2 * D].rearrange("p (h d) -> p d h", h=2),
                )
            neg_mean = small.tile([P, ROUND_HEADS], F32, name="neg_mean")
            nc.gpsimd.tensor_scalar(
                out=neg_mean[:], in0=stats[:, :, 1], scalar1=-1.0, scalar2=0.0, op0=ALU.mult, op1=ALU.add
            )
            var_eps = small.tile([P, ROUND_HEADS], F32, name="var_eps")
            nc.gpsimd.tensor_scalar(
                out=var_eps[:], in0=stats[:, :, 2], scalar1=1.0 / D, scalar2=EPS, op0=ALU.mult, op1=ALU.add
            )
            rstd = small.tile([P, ROUND_HEADS], F32, name="rstd")
            nc.gpsimd.tensor_tensor(out=rstd[:], in0=var_eps[:], in1=neg_half[:], op=ALU.pow)
            shift = small.tile([P, ROUND_HEADS], F32, name="shift")
            nc.gpsimd.tensor_tensor(out=shift[:], in0=neg_mean[:], in1=rstd[:], op=ALU.mult)
            rstd_of[n] = rstd
            shift_of[n] = shift

        def normalise(n):
            if n >= ROUNDS:
                return
            i, half = divmod(n, TILE_ROUNDS)
            norm = norm_pool.tile([P, ROUND_HEADS, PAIR, P], F32, name="norm")
            for h in range(ROUND_HEADS):
                first_col = half * ROUND_K + h * D
                nc.scalar.activation(
                    out=norm[:, h, :, :],
                    in_=ret_tiles[i][:, first_col : first_col + D].rearrange("p (q e) -> p e q", e=PAIR),
                    func=ACT.Identity,
                    scale=rstd_of[n][:, h : h + 1],
                    bias=shift_of[n][:, h : h + 1],
                )
            norm_of[n] = norm

        def transposes(n):
            if n >= ROUNDS:
                return
            i, half = divmod(n, TILE_ROUNDS)
            norm_T = [psum_norm.tile([P, PACK, P], F32, name="norm_T%d" % cr, tag="norm_T") for cr in range(ROUND_PASSES)]
            for cr in range(ROUND_PASSES):
                for t in range(PACK):
                    u, e = divmod(t, PAIR)
                    nc.tensor.transpose(norm_T[cr][:, t, :], norm_of[n][:, cr * HALVES + u, e, :], ident_f32[:])
            g_T = psum_g.tile([P, HALVES * WORDS], F32, name="g_T")
            g_words = g_tiles[i][:].bitcast(F32)
            for u in range(HALVES):
                for cr in range(ROUND_PASSES):
                    first_word = (half * ROUND_K + (cr * HALVES + u) * D) // PAIR
                    nc.tensor.transpose(
                        g_T[:, u * WORDS + cr * P : u * WORDS + (cr + 1) * P],
                        g_words[:, first_word : first_word + P],
                        ident_f32[:],
                    )
            norm_T_of[n] = norm_T
            g_T_of[n] = g_T

        def affine_and_silu(n):
            if n >= ROUNDS:
                return
            half = n % TILE_ROUNDS
            rn_T = kmajor.tile([P, PACK, WORDS], F32, name="rn_T")
            for cr in range(ROUND_PASSES):
                for t in range(PACK):
                    b = (half * ROUND_PASSES + cr) * PACK + t
                    nc.scalar.activation(
                        out=rn_T[:, t, cr * P : (cr + 1) * P], in_=norm_T_of[n][cr][:, t, :], func=ACT.Identity,
                        scale=affine_cols[:, b : b + 1], bias=affine_cols[:, K_BLOCKS + b : K_BLOCKS + b + 1],
                    )
            silu_T = kmajor.tile([P, PACK, WORDS], F32, name="silu_T")
            nc.scalar.activation(
                out=silu_T[:].rearrange("p (u e) x -> p u e x", e=PAIR),
                in_=g_T_of[n][:].bitcast(BF16).rearrange("p (u x e) -> p u e x", u=HALVES, e=PAIR),
                func=ACT.Silu,
            )
            rn_T_of[n] = rn_T
            silu_T_of[n] = silu_T

        def gate_product(n):
            if n < 0 or n >= ROUNDS:
                return
            gate_grouped = kmajor.tile([P, WORDS, PACK], BF16, name="gate_grouped", align_bytes=64)
            nc.vector.tensor_tensor(
                out=gate_grouped[:].rearrange("p (n i) t -> p n t i", i=4),
                in0=rn_T_of[n][:].rearrange("p t (n i) -> p n t i", i=4),
                in1=silu_T_of[n][:].rearrange("p t (n i) -> p n t i", i=4),
                op=ALU.mult,
            )
            gate_grouped_of[n] = gate_grouped

        def quantise_gate(n):
            if n < 0 or n >= ROUNDS:
                return
            nc.vector.quantize_mx(
                out=gate_codes[:, n, :].bitcast(FP8X4),
                scales=gate_scales[:, n, :],
                in_=gate_grouped_of[n][:].rearrange("p x t -> p (x t)"),
            )

        def regroup_w_piece(k):
            if k >= W_PIECES:
                return
            v = VECTOR_COLS
            grouped = w_grouped_pool.tile([P, W_COLS, PACK], BF16, name="grouped", align_bytes=64)
            nc.vector.tensor_copy(
                out=grouped[:, 0:v, :].rearrange("p (n i) t -> p n t i", i=4),
                in_=raw_tiles[k][:, :, 0:v].rearrange("p t (n i) -> p n t i", i=4),
            )
            nc.scalar.copy(
                out=grouped[:, v:W_COLS, :].rearrange("p (n i) t -> p n t i", i=4),
                in_=raw_tiles[k][:, :, v:W_COLS].rearrange("p t (n i) -> p n t i", i=4),
            )
            grouped_tiles[k] = grouped

        def quantise_w_piece(k):
            if k < 0 or k >= W_PIECES:
                return
            jj, c = divmod(k, PASSES)
            n_cols = slice(jj * W_COLS, (jj + 1) * W_COLS)
            nc.vector.quantize_mx(
                out=w_codes[:, c, n_cols].bitcast(FP8X4),
                scales=w_scales[:, c, n_cols],
                in_=grouped_tiles[k][:].rearrange("p n t -> p (n t)"),
            )

        def multiply(m):
            if m < 0 or m >= UNITS:
                return []
            i, jj = divmod(m, E // W_COLS)
            products = []
            for j in range(jj * UNIT_TILES, (jj + 1) * UNIT_TILES):
                n_cols = slice(j * N_TILE, (j + 1) * N_TILE)
                acc = psum_acc.tile([P, N_TILE], F32, name="acc")
                for c in range(PASSES):
                    half, cr = divmod(c, ROUND_PASSES)
                    made_in = i * TILE_ROUNDS + half
                    nc.tensor.matmul_mx(
                        out=acc[:],
                        lhsT=gate_codes[:, made_in, cr * P : (cr + 1) * P].bitcast(FP8X4),
                        lhsT_scale=gate_scales[:, made_in, cr * P : (cr + 1) * P],
                        rhs=w_codes[:, c, n_cols].bitcast(FP8X4),
                        rhs_scale=w_scales[:, c, n_cols],
                        start=(c == 0),
                        stop=(c == PASSES - 1),
                    )
                products.append((acc, slice(i * P, (i + 1) * P), n_cols))
            return products

        def add_bias_and_store(products):
            for acc, tokens, n_cols in products:
                result = out_pool.tile([P, N_TILE], F32, name="result")
                nc.vector.tensor_tensor(out=result[:], in0=acc[:], in1=bias_all[:, n_cols], op=ALU.add)
                nc.sync.dma_start(out=out_rows[tokens, n_cols], in_=result[:])

        for n in range(STATS_AHEAD):
            statistics(n)
        affine_ps = psum_g.tile([P, HALVES * WORDS], F32, tag="g_T")
        nc.tensor.transpose(affine_ps[:, 0:P], affine_rows[:].bitcast(F32), ident_f32[:])
        nc.vector.tensor_copy(out=affine_cols[:], in_=affine_ps[:, 0 : 2 * HEADS].bitcast(BF16))
        normalise(0)

        products = []
        for n in range(ROUNDS + UNIT_LAG + 1):
            statistics(n + STATS_AHEAD)
            transposes(n)
            normalise(n + 1)
            affine_and_silu(n)
            gate_product(n - 1)
            add_bias_and_store(products)
            quantise_gate(n - 1)
            first = n * PIECES_PER_STEP
            for k in range(first - PIECES_PER_STEP, first):
                quantise_w_piece(k)
            for k in range(first, first + PIECES_PER_STEP):
                regroup_w_piece(k)
            for k in range(first + RAW_PIECES, first + RAW_PIECES + PIECES_PER_STEP):
                load_w_piece(k)
            load_tokens(ret_rows, ret_tiles, n + 3, "ret_t")
            load_tokens(g_rows, g_tiles, n + 2, "g_t")
            if n == 1:
                nc.sync.dma_start(out=bias_all[:], in_=b_o.partition_broadcast(P))
            products = multiply(n - UNIT_LAG)
